import numpy as np
import ml_dtypes


def mxq(x, axis, fmt="e4m3"):
    dtype, down = {"e4m3": (ml_dtypes.float8_e4m3fn, 7), "e5m2": (ml_dtypes.float8_e5m2, 14)}[fmt]
    v = np.moveaxis(np.asarray(x, np.float32).astype(ml_dtypes.bfloat16).astype(np.float64), axis, -1)
    blocks = v.reshape(v.shape[:-1] + (-1, 32))
    amax = np.abs(blocks).max(-1, keepdims=True)
    byte = np.maximum(np.where(amax > 0, np.frexp(amax)[1] - 1 + 127, 0) - down, 1)
    scale = np.exp2(byte - 127.0)
    codes = (blocks / scale).astype(np.float32).astype(dtype).astype(np.float64)
    return np.moveaxis((codes * scale).reshape(v.shape), -1, axis)


WIDE = False


def mx_kscale(k):
    if not WIDE:
        return np.ones(k)
    levels = np.array([10, -10, 5, -5, 0])
    a = np.random.permutation(np.resize(levels, k // 512 * 4)).reshape(k // 512, 4)
    idx = np.arange(k)
    return np.exp2(a[idx // 512, idx % 128 // 32])


BF16 = ml_dtypes.bfloat16


def bf(x):
    return np.asarray(x, np.float32).astype(BF16)


def f64(x):
    return np.asarray(x).astype(np.float64)


B, S, D, F, N = 2, 1024, 1024, 1024, 1024
SPARSITY = 0.1


def make_theta_sign(d1, d2, gain, row, col):
    mask = np.random.random((d1, d2)) < SPARSITY
    mag = np.abs(np.random.standard_normal((d1, d2))) * gain / np.sqrt(SPARSITY * d1)
    th = np.where(mask, mag, -mag) / row[:, None] * col
    sign = np.where(np.random.random((d1, d2)) < 0.5, -1.0, 1.0)
    return bf(th), bf(sign)


def setup_inputs():
    s, t = mx_kscale(D), mx_kscale(F)
    x = bf(np.random.standard_normal((B, S, D)) * s)
    th1, sign1 = make_theta_sign(D, F, 1.0, s, t)
    th2, sign2 = make_theta_sign(F, N, 1.4, t, np.ones(N))
    return {"x": x, "th1": th1, "sign1": sign1, "th2": th2, "sign2": sign2, "relu": 1}


def reference(x, th1, sign1, th2, sign2, relu):
    x = f64(x)
    for th, sign in ((f64(th1), f64(sign1)), (f64(th2), f64(sign2))):
        w = th * sign * (th > 0)
        x = mxq(x, 2, "e4m3") @ mxq(w, 0, "e4m3")
        if relu:
            x = np.maximum(x, 0.0)
    return x

@@ -1,0 +1,194 @@
+from contextlib import ExitStack
+
+import concourse.mybir as mybir
+from concourse.masks import make_identity
+
+F32 = mybir.dt.float32
+BF16 = mybir.dt.bfloat16
+U32 = mybir.dt.uint32
+U8 = mybir.dt.uint8
+FP8X4 = mybir.dt.float8_e4m3fn_x4
+RELU = mybir.ActivationFunctionType.Relu
+MAX = mybir.AluOpType.max
+MULT = mybir.AluOpType.mult
+
+P = 128
+FLOPS = 2 * 2 * 2048 * 1024 * 1024
+MANUAL = True
+
+
+PJ = {"prog":[["T",0],["DT",0,"s"],["T",1],["DT",1,"s"],["QX",0],["BW",[1,0,0],0,512],["QW",[1,0,0],0,512],["BW",[1,1,0],0,256],["QW",[1,1,0],0,256],["BW",[1,1,0],256,256],["QW",[1,1,0],256,256],["T",2],["DT",2,"s"],["T",3],["DT",3,"s"],["QX",1],["L1",0,0,0,2],["L1",1,0,0,2],["L1",0,0,2,4],["DH",0,0,"s"],["L1",1,0,2,4],["DH",1,0,"v"],["T",4],["DT",4,"s"],["T",5],["DT",5,"v"],["T",6],["DT",6,"s"],["T",7],["DT",7,"s"],["QX",2],["BW",[1,0,1],0,256],["QX",3],["BW",[1,0,1],256,256],["L1",2,0,0,4],["DH",2,0,"s"],["L1",3,0,0,4],["DH",3,0,"s"],["L1",4,0,0,4],["DH",4,0,"s"],["L1",5,0,0,4],["DH",5,0,"s"],["T",8],["DT",8,"s"],["T",9],["DT",9,"v"],["T",10],["DT",10,"s"],["T",11],["DT",11,"s"],["QX",4],["QW",[1,0,1],0,512],["QX",5],["QH",0,0],["L1",6,0,0,4],["DH",6,0,"s"],["L1",7,0,0,4],["DH",7,0,"s"],["L1",8,0,0,4],["DH",8,0,"s"],["L1",9,0,0,4],["DH",9,0,"s"],["QH",0,1],["BW",[1,1,1],0,256],["T",12],["DT",12,"s"],["T",13],["DT",13,"s"],["T",14],["DT",14,"s"],["T",15],["DT",15,"v"],["QX",6],["QX",7],["BW",[1,1,1],256,256],["QW",[1,1,1],0,512],["L1",10,0,0,4],["DH",10,0,"s"],["L1",11,0,0,4],["DH",11,0,"s"],["L1",12,0,0,4],["DH",12,0,"s"],["L1",13,0,0,4],["DH",13,0,"s"],["L1",14,0,0,4],["DH",14,0,"s"],["L1",15,0,0,4],["DH",15,0,"s"],["BW",[2,0,0],0,256],["BW",[2,0,0],256,256],["QW",[2,0,0],0,512],["L1",0,1,0,4],["DH",0,1,"s"],["L1",1,1,0,4],["DH",1,1,"s"],["L1",2,1,0,4],["DH",2,1,"s"],["L1",3,1,0,4],["DH",3,1,"s"],["L1",4,1,0,4],["DH",4,1,"s"],["BW",[2,1,0],0,256],["L1",5,1,0,4],["DH",5,1,"s"],["QH",1,0],["BW",[2,1,0],256,256],["QW",[2,1,0],0,512],["L1",6,1,0,4],["DH",6,1,"s"],["L1",7,1,0,4],["DH",7,1,"s"],["L1",8,1,0,4],["DH",8,1,"s"],["QH",1,1],["L1",9,1,0,4],["DH",9,1,"s"],["L1",10,1,0,4],["DH",10,1,"s"],["L1",11,1,0,4],["DH",11,1,"s"],["QH",0,2],["C",0,0],["DC",0,0,"s"],["C",1,0],["DC",1,0,"s"],["BW",[2,0,1],0,256],["C",2,0],["DC",2,0,"s"],["C",3,0],["DC",3,0,"v"],["C",4,0],["DC",4,0,"s"],["BW",[2,0,1],256,256],["C",5,0],["DC",5,0,"s"],["C",6,0],["DC",6,0,"s"],["QH",1,2],["C",7,0],["DC",7,0,"v"],["QW",[2,0,1],0,512],["L1",12,1,0,4],["DH",12,1,"s"],["QH",0,3],["BW",[2,1,1],0,256],["L1",13,1,0,4],["DH",13,1,"s"],["L1",14,1,0,4],["DH",14,1,"s"],["BW",[2,1,1],256,256],["L1",15,1,0,4],["DH",15,1,"s"],["QW",[2,1,1],0,512],["C",8,0],["DC",8,0,"s"],["C",9,0],["DC",9,0,"s"],["QH",1,3],["C",10,0],["DC",10,0,"v"],["C",11,0],["DC",11,0,"s"],["C",12,0],["DC",12,0,"s"],["C",13,0],["DC",13,0,"v"],["C",14,0],["DC",14,0,"s"],["C",15,0],["DC",15,0,"s"],["C",0,1],["DC",0,1,"s"],["C",1,1],["DC",1,1,"v"],["C",2,1],["DC",2,1,"s"],["C",3,1],["DC",3,1,"v"],["C",4,1],["DC",4,1,"s"],["C",5,1],["DC",5,1,"v"],["C",6,1],["DC",6,1,"s"],["C",7,1],["DC",7,1,"v"],["C",8,1],["DC",8,1,"s"],["C",9,1],["DC",9,1,"v"],["C",10,1],["DC",10,1,"s"],["C",11,1],["DC",11,1,"v"],["C",12,1],["DC",12,1,"s"],["C",13,1],["DC",13,1,"v"],["C",14,1],["DC",14,1,"s"],["C",15,1],["DC",15,1,"v"]],"loads":[["x",0,0,2],["w1",0,0],["w1",1,0],["x",0,2,2],["x",1,0,4],["w1",0,1],["x",2,0,4],["x",3,0,4],["w1",1,1],["w2",0,0],["w2",1,0],["w2",0,1],["w2",1,1]],"hgbufs":6}
+
+
+def make_program():
+    return [tuple(tuple(a) if isinstance(a, list) else a for a in t) for t in PJ["prog"]]
+
+
+def tile_sparse_connect_kernel(tc, x, th1, sign1, th2, sign2, relu, out):
+    nc = tc.nc
+    xv = x.flatten_outer_dims().rearrange("(b p j) d -> b p j d", p=P, j=4)
+    ov = out.flatten_outer_dims().rearrange("(b p j) n -> b p j n", p=P, j=4)
+    w1v = {"t": th1.rearrange("(w q e) f -> w q e f", w=4, e=2), "s": sign1.rearrange("(w q e) f -> w q e f", w=4, e=2)}
+    w2v = {"t": th2.rearrange("(a p) n -> p a n", p=P), "s": sign2.rearrange("(a p) n -> p a n", p=P)}
+    with ExitStack() as ctx:
+        raw = ctx.enter_context(tc.tile_pool(name="raw", bufs=1))
+        keep = ctx.enter_context(tc.tile_pool(name="keep", bufs=1))
+        stage = ctx.enter_context(tc.tile_pool(name="stage", bufs=3))
+        outp = ctx.enter_context(tc.tile_pool(name="outp", bufs=8))
+        psum = ctx.enter_context(tc.psum_pool(name="psum", bufs=8))
+        if MANUAL:
+            ctx.enter_context(tc.manual_schedule())
+
+        ident = raw.tile([P, P], F32, name="ident")
+        make_identity(nc, ident[:])
+
+        xr = {}
+        wraw = {}
+
+        def load_x(b, j0, nj):
+            t = raw.tile([P, nj, 1024], BF16, name="xr%d_%d" % (b, j0))
+            nc.sync.dma_start(out=t[:], in_=xv[b, :, j0:j0 + nj, :])
+            for j in range(nj):
+                xr[4 * b + j0 + j] = t[:, j, :]
+
+        def load_w1(g, G):
+            for kind in ("t", "s"):
+                t = raw.tile([P, 4, 512], BF16, name="w1%s%d%d" % (kind, g, G))
+                for u in range(2):
+                    nc.sync.dma_start(out=t[:, 2 * u:2 * u + 2, :], in_=w1v[kind][2 * g + u, :, :, 512 * G:512 * G + 512])
+                wraw[(1, g, G, kind)] = t
+
+        def load_w2(G, n):
+            for kind in ("t", "s"):
+                t = raw.tile([P, 4, 512], BF16, name="w2%s%d%d" % (kind, G, n))
+                nc.sync.dma_start(out=t[:], in_=w2v[kind][:, 4 * G:4 * G + 4, 512 * n:512 * n + 512])
+                wraw[(2, G, n, kind)] = t
+
+        for ld in PJ["loads"]:
+            if ld[0] == "x":
+                load_x(ld[1], ld[2], ld[3])
+            elif ld[0] == "w1":
+                load_w1(ld[1], ld[2])
+            else:
+                load_w2(ld[1], ld[2])
+
+        wc = {}
+        ws = {}
+        for key in [(1, g, G) for g in range(2) for G in range(2)] + [(2, G, n) for G in range(2) for n in range(2)]:
+            wc[key] = keep.tile([P, 512], U32, name="wc%d%d%d" % key, align_bytes=64)
+            ws[key] = keep.tile([P, 512], U8, name="ws%d%d%d" % key, align_bytes=64)
+        xc = [keep.tile([P, 512], U32, name="xc%d" % k, align_bytes=64) for k in range(8)]
+        xs = [keep.tile([P, 512], U8, name="xs%d" % k, align_bytes=64) for k in range(8)]
+        hc = [[keep.tile([P, 512], U32, name="hc%d%d" % (G, b), align_bytes=64) for b in range(4)] for G in range(2)]
+        hs = [[keep.tile([P, 512], U8, name="hs%d%d" % (G, b), align_bytes=64) for b in range(4)] for G in range(2)]
+        xg = {}
+        hg = {}
+        wg = {}
+
+        def drain_relu(eng, dst, src):
+            if eng == "s":
+                nc.scalar.activation(out=dst, in_=src, func=RELU)
+            else:
+                nc.vector.tensor_scalar_max(out=dst, in0=src, scalar1=0.0)
+
+        tb = {}
+
+        def op_T(i):
+            bank = psum.tile([P, 512], F32, tag="bank", name="bank")
+            tb[i] = bank
+            src = xr[i].bitcast(F32)
+            for w in range(4):
+                nc.tensor.transpose(bank[:, 128 * w:128 * w + 128], src[:, 128 * w:128 * w + 128], ident[:])
+
+        def op_DT(i, eng):
+            if (i // 2) not in xg:
+                xg[i // 2] = stage.tile([P, 2048], BF16, tag="xg", name="xg", align_bytes=64, bufs=PJ.get("xgbufs", 3))
+            dst = xg[i // 2][:].bitcast(F32).rearrange("q (j g r u) -> q j g r u", j=2, g=2, u=2)[:, i % 2]
+            src2 = tb[i][:].rearrange("q (g u r) -> q g r u", g=2, u=2)
+            if eng == "s":
+                nc.scalar.copy(out=dst, in_=src2)
+            else:
+                nc.vector.tensor_copy(out=dst, in_=src2)
+
+        def op_QX(k):
+            nc.vector.quantize_mx(out=xc[k][:].bitcast(FP8X4), scales=xs[k][:], in_=xg[k][:])
+
+        def op_BW(key, c0, ncol):
+            if c0 == 0 or key == (1, 1, 0):
+                wg[key] = stage.tile([P, 512 if key != (1, 1, 0) else 256, 4], BF16, tag="wg", name="wg", align_bytes=64)
+            o0 = 0 if key == (1, 1, 0) else c0
+            nc.vector.scalar_tensor_tensor(
+                out=wg[key][:, o0:o0 + ncol, :],
+                in0=wraw[key + ("t",)][:, :, c0:c0 + ncol].rearrange("q t c -> q c t"),
+                scalar=0.0,
+                in1=wraw[key + ("s",)][:, :, c0:c0 + ncol].rearrange("q t c -> q c t"),
+                op0=MAX, op1=MULT)
+
+        def op_QW(key, c0, ncol):
+            nc.vector.quantize_mx(out=wc[key][:, c0:c0 + ncol].bitcast(FP8X4), scales=ws[key][:, c0:c0 + ncol],
+                                  in_=wg[key][:].rearrange("q c t -> q (c t)"))
+
+        banks = {}
+
+        def op_L1(i, G, t0=0, t1=4):
+            if t0 == 0:
+                banks[(i, G)] = psum.tile([P, 512], F32, tag="bank", name="bank")
+            bank = banks[(i, G)]
+            for t in range(t0, t1):
+                for g in range(2):
+                    o = ((i % 2) * 2 + g) * 128
+                    nc.tensor.matmul_mx(out=bank[:, 128 * t:128 * t + 128],
+                                        lhsT=wc[(1, g, G)][:, 128 * t:128 * t + 128].bitcast(FP8X4),
+                                        lhsT_scale=ws[(1, g, G)][:, 128 * t:128 * t + 128],
+                                        rhs=xc[i // 2][:, o:o + 128].bitcast(FP8X4),
+                                        rhs_scale=xs[i // 2][:, o:o + 128],
+                                        start=(g == 0), stop=(g == 1))
+
+        def op_DH(i, G, eng):
+            if (G, i // 4) not in hg:
+                hg[(G, i // 4)] = stage.tile([P, 4, 128, 4], BF16, tag="hg", name="hg", align_bytes=64, bufs=PJ.get("hgbufs", 5))
+            drain_relu(eng, hg[(G, i // 4)][:, i % 4], banks[(i, G)][:].rearrange("p (t r) -> p r t", t=4))
+
+        def op_QH(G, b):
+            nc.vector.quantize_mx(out=hc[G][b][:].bitcast(FP8X4), scales=hs[G][b][:],
+                                  in_=hg[(G, b)][:].rearrange("p j r t -> p (j r t)"))
+
+        ob = {}
+
+        def op_L2(i, n):
+            bank = psum.tile([P, 512], F32, tag="bank", name="bank")
+            ob[(i, n)] = bank
+            o = (i % 4) * 128
+            for G in range(2):
+                nc.tensor.matmul_mx(out=bank[:], lhsT=hc[G][i // 4][:, o:o + 128].bitcast(FP8X4),
+                                    lhsT_scale=hs[G][i // 4][:, o:o + 128],
+                                    rhs=wc[(2, G, n)][:].bitcast(FP8X4), rhs_scale=ws[(2, G, n)][:],
+                                    start=(G == 0), stop=(G == 1))
+
+        def op_DC(i, n, eng):
+            ot = outp.tile([P, 512], F32, tag="ot", name="ot")
+            drain_relu(eng, ot[:], ob[(i, n)][:])
+            nc.sync.dma_start(out=ov[i // 4, :, i % 4, 512 * n:512 * n + 512], in_=ot[:])
+
+        for ti, tok in enumerate(make_program()):
+            k = tok[0]
+            if k == "T":
+                op_T(tok[1])
+            elif k == "DT":
+                op_DT(tok[1], tok[2])
+            elif k == "QX":
+                op_QX(tok[1])
+            elif k == "BW":
+                op_BW(tok[1], tok[2], tok[3])
+            elif k == "QW":
+                op_QW(tok[1], tok[2], tok[3])
+            elif k == "L1":
+                op_L1(tok[1], tok[2], tok[3], tok[4])
+            elif k == "DH":
+                op_DH(tok[1], tok[2], tok[3])
+            elif k == "QH":
+                op_QH(tok[1], tok[2])
+            elif k == "C":
+                op_L2(tok[1], tok[2])
+            else:
+                op_DC(tok[1], tok[2], tok[3])

@@ -14,7 +14,7 @@ MULT = mybir.AluOpType.mult
 
 P = 128
 FLOPS = 2 * 2 * 2048 * 1024 * 1024
-MANUAL = True
+MANUAL = False
 
 
 PJ = {"prog":[["T",0],["DT",0,"s"],["T",1],["DT",1,"s"],["QX",0],["BW",[1,0,0],0,512],["QW",[1,0,0],0,512],["BW",[1,1,0],0,256],["QW",[1,1,0],0,256],["BW",[1,1,0],256,256],["QW",[1,1,0],256,256],["T",2],["DT",2,"s"],["T",3],["DT",3,"s"],["QX",1],["L1",0,0,0,2],["L1",1,0,0,2],["L1",0,0,2,4],["DH",0,0,"s"],["L1",1,0,2,4],["DH",1,0,"v"],["T",4],["DT",4,"s"],["T",5],["DT",5,"v"],["T",6],["DT",6,"s"],["T",7],["DT",7,"s"],["QX",2],["BW",[1,0,1],0,256],["QX",3],["BW",[1,0,1],256,256],["L1",2,0,0,4],["DH",2,0,"s"],["L1",3,0,0,4],["DH",3,0,"s"],["L1",4,0,0,4],["DH",4,0,"s"],["L1",5,0,0,4],["DH",5,0,"s"],["T",8],["DT",8,"s"],["T",9],["DT",9,"v"],["T",10],["DT",10,"s"],["T",11],["DT",11,"s"],["QX",4],["QW",[1,0,1],0,512],["QX",5],["QH",0,0],["L1",6,0,0,4],["DH",6,0,"s"],["L1",7,0,0,4],["DH",7,0,"s"],["L1",8,0,0,4],["DH",8,0,"s"],["L1",9,0,0,4],["DH",9,0,"s"],["QH",0,1],["BW",[1,1,1],0,256],["T",12],["DT",12,"s"],["T",13],["DT",13,"s"],["T",14],["DT",14,"s"],["T",15],["DT",15,"v"],["QX",6],["QX",7],["BW",[1,1,1],256,256],["QW",[1,1,1],0,512],["L1",10,0,0,4],["DH",10,0,"s"],["L1",11,0,0,4],["DH",11,0,"s"],["L1",12,0,0,4],["DH",12,0,"s"],["L1",13,0,0,4],["DH",13,0,"s"],["L1",14,0,0,4],["DH",14,0,"s"],["L1",15,0,0,4],["DH",15,0,"s"],["BW",[2,0,0],0,256],["BW",[2,0,0],256,256],["QW",[2,0,0],0,512],["L1",0,1,0,4],["DH",0,1,"s"],["L1",1,1,0,4],["DH",1,1,"s"],["L1",2,1,0,4],["DH",2,1,"s"],["L1",3,1,0,4],["DH",3,1,"s"],["L1",4,1,0,4],["DH",4,1,"s"],["BW",[2,1,0],0,256],["L1",5,1,0,4],["DH",5,1,"s"],["QH",1,0],["BW",[2,1,0],256,256],["QW",[2,1,0],0,512],["L1",6,1,0,4],["DH",6,1,"s"],["L1",7,1,0,4],["DH",7,1,"s"],["L1",8,1,0,4],["DH",8,1,"s"],["QH",1,1],["L1",9,1,0,4],["DH",9,1,"s"],["L1",10,1,0,4],["DH",10,1,"s"],["L1",11,1,0,4],["DH",11,1,"s"],["QH",0,2],["C",0,0],["DC",0,0,"s"],["C",1,0],["DC",1,0,"s"],["BW",[2,0,1],0,256],["C",2,0],["DC",2,0,"s"],["C",3,0],["DC",3,0,"v"],["C",4,0],["DC",4,0,"s"],["BW",[2,0,1],256,256],["C",5,0],["DC",5,0,"s"],["C",6,0],["DC",6,0,"s"],["QH",1,2],["C",7,0],["DC",7,0,"v"],["QW",[2,0,1],0,512],["L1",12,1,0,4],["DH",12,1,"s"],["QH",0,3],["BW",[2,1,1],0,256],["L1",13,1,0,4],["DH",13,1,"s"],["L1",14,1,0,4],["DH",14,1,"s"],["BW",[2,1,1],256,256],["L1",15,1,0,4],["DH",15,1,"s"],["QW",[2,1,1],0,512],["C",8,0],["DC",8,0,"s"],["C",9,0],["DC",9,0,"s"],["QH",1,3],["C",10,0],["DC",10,0,"v"],["C",11,0],["DC",11,0,"s"],["C",12,0],["DC",12,0,"s"],["C",13,0],["DC",13,0,"v"],["C",14,0],["DC",14,0,"s"],["C",15,0],["DC",15,0,"s"],["C",0,1],["DC",0,1,"s"],["C",1,1],["DC",1,1,"v"],["C",2,1],["DC",2,1,"s"],["C",3,1],["DC",3,1,"v"],["C",4,1],["DC",4,1,"s"],["C",5,1],["DC",5,1,"v"],["C",6,1],["DC",6,1,"s"],["C",7,1],["DC",7,1,"v"],["C",8,1],["DC",8,1,"s"],["C",9,1],["DC",9,1,"v"],["C",10,1],["DC",10,1,"s"],["C",11,1],["DC",11,1,"v"],["C",12,1],["DC",12,1,"s"],["C",13,1],["DC",13,1,"v"],["C",14,1],["DC",14,1,"s"],["C",15,1],["DC",15,1,"v"]],"loads":[["x",0,0,2],["w1",0,0],["w1",1,0],["x",0,2,2],["x",1,0,4],["w1",0,1],["x",2,0,4],["x",3,0,4],["w1",1,1],["w2",0,0],["w2",1,0],["w2",0,1],["w2",1,1]],"hgbufs":6}
@@ -100,6 +100,12 @@ def tile_sparse_connect_kernel(tc, x, th1, sign1, th2, sign2, relu, out):
             for w in range(4):
                 nc.tensor.transpose(bank[:, 128 * w:128 * w + 128], src[:, 128 * w:128 * w + 128], ident[:])
 
+        def op_warm(key, count):
+            src = wraw[key + ("t",)]
+            bank = psum.tile([P, 512], F32, tag="bank", name="bank")
+            for r in range(count):
+                nc.tensor.matmul(out=bank[:], lhsT=src[:, r % 4, 0:128], rhs=src[:, r % 4, :], start=True, stop=True)
+
         def op_DT(i, eng):
             if (i // 2) not in xg:
                 xg[i // 2] = stage.tile([P, 2048], BF16, tag="xg", name="xg", align_bytes=64, bufs=PJ.get("xgbufs", 3))
@@ -174,6 +180,11 @@ def tile_sparse_connect_kernel(tc, x, th1, sign1, th2, sign2, relu, out):
             k = tok[0]
             if k == "T":
                 op_T(tok[1])
+            elif k == "TB":
+                for i in range(tok[1], tok[1] + tok[2]):
+                    op_T(i)
+            elif k == "W":
+                op_warm(tok[1], tok[2])
             elif k == "DT":
                 op_DT(tok[1], tok[2])
             elif k == "QX":

@@ -14,10 +14,10 @@ MULT = mybir.AluOpType.mult
 
 P = 128
 FLOPS = 2 * 2 * 2048 * 1024 * 1024
-MANUAL = False
+MANUAL = True
 
 
-PJ = {"prog":[["T",0],["DT",0,"s"],["T",1],["DT",1,"s"],["QX",0],["BW",[1,0,0],0,512],["QW",[1,0,0],0,512],["BW",[1,1,0],0,256],["QW",[1,1,0],0,256],["BW",[1,1,0],256,256],["QW",[1,1,0],256,256],["T",2],["DT",2,"s"],["T",3],["DT",3,"s"],["QX",1],["L1",0,0,0,2],["L1",1,0,0,2],["L1",0,0,2,4],["DH",0,0,"s"],["L1",1,0,2,4],["DH",1,0,"v"],["T",4],["DT",4,"s"],["T",5],["DT",5,"v"],["T",6],["DT",6,"s"],["T",7],["DT",7,"s"],["QX",2],["BW",[1,0,1],0,256],["QX",3],["BW",[1,0,1],256,256],["L1",2,0,0,4],["DH",2,0,"s"],["L1",3,0,0,4],["DH",3,0,"s"],["L1",4,0,0,4],["DH",4,0,"s"],["L1",5,0,0,4],["DH",5,0,"s"],["T",8],["DT",8,"s"],["T",9],["DT",9,"v"],["T",10],["DT",10,"s"],["T",11],["DT",11,"s"],["QX",4],["QW",[1,0,1],0,512],["QX",5],["QH",0,0],["L1",6,0,0,4],["DH",6,0,"s"],["L1",7,0,0,4],["DH",7,0,"s"],["L1",8,0,0,4],["DH",8,0,"s"],["L1",9,0,0,4],["DH",9,0,"s"],["QH",0,1],["BW",[1,1,1],0,256],["T",12],["DT",12,"s"],["T",13],["DT",13,"s"],["T",14],["DT",14,"s"],["T",15],["DT",15,"v"],["QX",6],["QX",7],["BW",[1,1,1],256,256],["QW",[1,1,1],0,512],["L1",10,0,0,4],["DH",10,0,"s"],["L1",11,0,0,4],["DH",11,0,"s"],["L1",12,0,0,4],["DH",12,0,"s"],["L1",13,0,0,4],["DH",13,0,"s"],["L1",14,0,0,4],["DH",14,0,"s"],["L1",15,0,0,4],["DH",15,0,"s"],["BW",[2,0,0],0,256],["BW",[2,0,0],256,256],["QW",[2,0,0],0,512],["L1",0,1,0,4],["DH",0,1,"s"],["L1",1,1,0,4],["DH",1,1,"s"],["L1",2,1,0,4],["DH",2,1,"s"],["L1",3,1,0,4],["DH",3,1,"s"],["L1",4,1,0,4],["DH",4,1,"s"],["BW",[2,1,0],0,256],["L1",5,1,0,4],["DH",5,1,"s"],["QH",1,0],["BW",[2,1,0],256,256],["QW",[2,1,0],0,512],["L1",6,1,0,4],["DH",6,1,"s"],["L1",7,1,0,4],["DH",7,1,"s"],["L1",8,1,0,4],["DH",8,1,"s"],["QH",1,1],["L1",9,1,0,4],["DH",9,1,"s"],["L1",10,1,0,4],["DH",10,1,"s"],["L1",11,1,0,4],["DH",11,1,"s"],["QH",0,2],["C",0,0],["DC",0,0,"s"],["C",1,0],["DC",1,0,"s"],["BW",[2,0,1],0,256],["C",2,0],["DC",2,0,"s"],["C",3,0],["DC",3,0,"v"],["C",4,0],["DC",4,0,"s"],["BW",[2,0,1],256,256],["C",5,0],["DC",5,0,"s"],["C",6,0],["DC",6,0,"s"],["QH",1,2],["C",7,0],["DC",7,0,"v"],["QW",[2,0,1],0,512],["L1",12,1,0,4],["DH",12,1,"s"],["QH",0,3],["BW",[2,1,1],0,256],["L1",13,1,0,4],["DH",13,1,"s"],["L1",14,1,0,4],["DH",14,1,"s"],["BW",[2,1,1],256,256],["L1",15,1,0,4],["DH",15,1,"s"],["QW",[2,1,1],0,512],["C",8,0],["DC",8,0,"s"],["C",9,0],["DC",9,0,"s"],["QH",1,3],["C",10,0],["DC",10,0,"v"],["C",11,0],["DC",11,0,"s"],["C",12,0],["DC",12,0,"s"],["C",13,0],["DC",13,0,"v"],["C",14,0],["DC",14,0,"s"],["C",15,0],["DC",15,0,"s"],["C",0,1],["DC",0,1,"s"],["C",1,1],["DC",1,1,"v"],["C",2,1],["DC",2,1,"s"],["C",3,1],["DC",3,1,"v"],["C",4,1],["DC",4,1,"s"],["C",5,1],["DC",5,1,"v"],["C",6,1],["DC",6,1,"s"],["C",7,1],["DC",7,1,"v"],["C",8,1],["DC",8,1,"s"],["C",9,1],["DC",9,1,"v"],["C",10,1],["DC",10,1,"s"],["C",11,1],["DC",11,1,"v"],["C",12,1],["DC",12,1,"s"],["C",13,1],["DC",13,1,"v"],["C",14,1],["DC",14,1,"s"],["C",15,1],["DC",15,1,"v"]],"loads":[["x",0,0,2],["w1",0,0],["w1",1,0],["x",0,2,2],["x",1,0,4],["w1",0,1],["x",2,0,4],["x",3,0,4],["w1",1,1],["w2",0,0],["w2",1,0],["w2",0,1],["w2",1,1]],"hgbufs":6}
+PJ = {"prog":[["TB",0,2],["DT",0,"s"],["W",[1,0,0],8],["DT",1,"s"],["QX",0],["BW",[1,0,0],0,512],["W",[1,1,0],4],["QW",[1,0,0],0,512],["BW",[1,1,0],0,256],["TB",2,2],["BW",[1,1,0],256,256],["DT",2,"s"],["DT",3,"s"],["QW",[1,1,0],0,256],["QW",[1,1,0],256,256],["QX",1],["L1",0,0,0,4],["L1",1,0,0,4],["DH",0,0,"s"],["TB",4,4],["DH",1,0,"s"],["L1",2,0,0,4],["DT",4,"s"],["DT",5,"v"],["L1",3,0,0,4],["DT",6,"s"],["DT",7,"v"],["QX",2],["DH",2,0,"s"],["TB",8,4],["DH",3,0,"s"],["QX",3],["BW",[1,0,1],0,256],["L1",4,0,0,4],["DT",8,"s"],["L1",5,0,0,4],["DT",9,"s"],["DT",10,"v"],["L1",6,0,0,4],["DT",11,"s"],["QX",4],["L1",7,0,0,4],["DH",4,0,"s"],["QX",5],["DH",5,0,"s"],["TB",12,4],["BW",[1,0,1],256,256],["DH",6,0,"s"],["DH",7,0,"s"],["L1",8,0,0,4],["QW",[1,0,1],0,512],["DT",12,"s"],["BW",[1,1,1],0,256],["L1",9,0,0,4],["DT",13,"s"],["L1",10,0,0,4],["DT",14,"s"],["QX",6],["L1",11,0,0,4],["DT",15,"s"],["DH",8,0,"s"],["QX",7],["L1",12,0,0,4],["DH",9,0,"s"],["BW",[1,1,1],256,256],["L1",13,0,0,4],["DH",10,0,"s"],["L1",14,0,0,4],["DH",11,0,"s"],["L1",15,0,0,4],["QW",[1,1,1],0,512],["DH",12,0,"s"],["BW",[2,0,0],0,256],["DH",13,0,"s"],["L1",0,1,0,4],["DH",14,0,"s"],["L1",1,1,0,4],["BW",[2,0,0],256,256],["DH",15,0,"s"],["L1",2,1,0,4],["DH",0,1,"s"],["L1",3,1,0,4],["DH",1,1,"s"],["QW",[2,0,0],0,512],["L1",4,1,0,4],["DH",2,1,"s"],["DH",3,1,"v"],["L1",5,1,0,4],["DH",4,1,"s"],["BW",[2,1,0],0,256],["L1",6,1,0,4],["DH",5,1,"s"],["L1",7,1,0,4],["BW",[2,1,0],256,256],["DH",6,1,"s"],["L1",8,1,0,4],["DH",7,1,"s"],["L1",9,1,0,4],["DH",8,1,"s"],["QW",[2,1,0],0,512],["L1",10,1,0,4],["DH",9,1,"s"],["QH",0,0],["L1",11,1,0,4],["DH",10,1,"s"],["QH",1,0],["DH",11,1,"s"],["QH",0,1],["C",0,0],["QH",1,1],["C",1,0],["DC",0,0,"s"],["QH",0,2],["C",2,0],["DC",1,0,"s"],["QH",1,2],["C",3,0],["DC",2,0,"s"],["QH",0,3],["C",4,0],["DC",3,0,"s"],["BW",[2,0,1],0,256],["C",5,0],["DC",4,0,"s"],["C",6,0],["DC",5,0,"s"],["BW",[2,0,1],256,256],["C",7,0],["DC",6,0,"s"],["L1",12,1,0,4],["DC",7,0,"s"],["L1",13,1,0,4],["QW",[2,0,1],0,512],["DH",12,1,"s"],["L1",14,1,0,4],["BW",[2,1,1],0,256],["DH",13,1,"s"],["L1",15,1,0,4],["DH",14,1,"s"],["BW",[2,1,1],256,256],["C",8,0],["DH",15,1,"s"],["C",9,0],["DC",8,0,"s"],["C",10,0],["QH",1,3],["DC",9,0,"s"],["C",11,0],["QW",[2,1,1],0,512],["DC",10,0,"s"],["C",12,0],["DC",11,0,"s"],["C",13,0],["DC",12,0,"s"],["C",14,0],["DC",13,0,"s"],["C",15,0],["DC",14,0,"s"],["C",0,1],["DC",15,0,"s"],["C",1,1],["DC",0,1,"s"],["C",2,1],["DC",1,1,"v"],["C",3,1],["DC",2,1,"s"],["C",4,1],["DC",3,1,"v"],["C",5,1],["DC",4,1,"s"],["C",6,1],["DC",5,1,"v"],["C",7,1],["DC",6,1,"s"],["C",8,1],["DC",7,1,"v"],["C",9,1],["DC",8,1,"s"],["C",10,1],["DC",9,1,"v"],["C",11,1],["DC",10,1,"s"],["C",12,1],["DC",11,1,"v"],["C",13,1],["DC",12,1,"s"],["C",14,1],["DC",13,1,"v"],["C",15,1],["DC",14,1,"s"],["DC",15,1,"v"]],"loads":[["x",0,0,2],["w1",0,0],["w1",1,0],["x",0,2,2],["x",1,0,4],["x",2,0,4],["w1",0,1],["x",3,0,4],["w1",1,1],["w2",0,0],["w2",1,0],["w2",0,1],["w2",1,1]],"hgbufs":7,"xgbufs":3}
 
 
 def make_program():
@@ -120,11 +120,10 @@ def tile_sparse_connect_kernel(tc, x, th1, sign1, th2, sign2, relu, out):
             nc.vector.quantize_mx(out=xc[k][:].bitcast(FP8X4), scales=xs[k][:], in_=xg[k][:])
 
         def op_BW(key, c0, ncol):
-            if c0 == 0 or key == (1, 1, 0):
-                wg[key] = stage.tile([P, 512 if key != (1, 1, 0) else 256, 4], BF16, tag="wg", name="wg", align_bytes=64)
-            o0 = 0 if key == (1, 1, 0) else c0
+            if key not in wg:
+                wg[key] = stage.tile([P, 512, 4], BF16, tag="wg", name="wg", align_bytes=64)
             nc.vector.scalar_tensor_tensor(
-                out=wg[key][:, o0:o0 + ncol, :],
+                out=wg[key][:, c0:c0 + ncol, :],
                 in0=wraw[key + ("t",)][:, :, c0:c0 + ncol].rearrange("q t c -> q c t"),
                 scalar=0.0,
                 in1=wraw[key + ("s",)][:, :, c0:c0 + ncol].rearrange("q t c -> q c t"),
@@ -132,7 +131,7 @@ def tile_sparse_connect_kernel(tc, x, th1, sign1, th2, sign2, relu, out):
 
         def op_QW(key, c0, ncol):
             nc.vector.quantize_mx(out=wc[key][:, c0:c0 + ncol].bitcast(FP8X4), scales=ws[key][:, c0:c0 + ncol],
-                                  in_=wg[key][:].rearrange("q c t -> q (c t)"))
+                                  in_=wg[key][:, c0:c0 + ncol, :].rearrange("q c t -> q (c t)"))
 
         banks = {}
 

@@ -13,192 +13,235 @@ MAX = mybir.AluOpType.max
 MULT = mybir.AluOpType.mult
 
 P = 128
-FLOPS = 2 * 2 * 2048 * 1024 * 1024
-MANUAL = True
+PACK = 4
+HALF = 512
+WIDTH = 1024
+TILES = 16
+FLOPS = 2 * 2 * TILES * P * WIDTH * WIDTH
 
-
-PJ = {"prog":[["TB",0,2],["DT",0,"s"],["W",[1,0,0],8],["DT",1,"s"],["QX",0],["BW",[1,0,0],0,512],["W",[1,1,0],4],["QW",[1,0,0],0,512],["BW",[1,1,0],0,256],["TB",2,2],["BW",[1,1,0],256,256],["DT",2,"s"],["DT",3,"s"],["QW",[1,1,0],0,256],["QW",[1,1,0],256,256],["QX",1],["L1",0,0,0,4],["L1",1,0,0,4],["DH",0,0,"s"],["TB",4,4],["DH",1,0,"s"],["L1",2,0,0,4],["DT",4,"s"],["DT",5,"v"],["L1",3,0,0,4],["DT",6,"s"],["DT",7,"v"],["QX",2],["DH",2,0,"s"],["TB",8,4],["DH",3,0,"s"],["QX",3],["BW",[1,0,1],0,256],["L1",4,0,0,4],["DT",8,"s"],["L1",5,0,0,4],["DT",9,"s"],["DT",10,"v"],["L1",6,0,0,4],["DT",11,"s"],["QX",4],["L1",7,0,0,4],["DH",4,0,"s"],["QX",5],["DH",5,0,"s"],["TB",12,4],["BW",[1,0,1],256,256],["DH",6,0,"s"],["DH",7,0,"s"],["L1",8,0,0,4],["QW",[1,0,1],0,512],["DT",12,"s"],["BW",[1,1,1],0,256],["L1",9,0,0,4],["DT",13,"s"],["L1",10,0,0,4],["DT",14,"s"],["QX",6],["L1",11,0,0,4],["DT",15,"s"],["DH",8,0,"s"],["QX",7],["L1",12,0,0,4],["DH",9,0,"s"],["BW",[1,1,1],256,256],["L1",13,0,0,4],["DH",10,0,"s"],["L1",14,0,0,4],["DH",11,0,"s"],["L1",15,0,0,4],["QW",[1,1,1],0,512],["DH",12,0,"s"],["BW",[2,0,0],0,256],["DH",13,0,"s"],["L1",0,1,0,4],["DH",14,0,"s"],["L1",1,1,0,4],["BW",[2,0,0],256,256],["DH",15,0,"s"],["L1",2,1,0,4],["DH",0,1,"s"],["L1",3,1,0,4],["DH",1,1,"s"],["QW",[2,0,0],0,512],["L1",4,1,0,4],["DH",2,1,"s"],["DH",3,1,"v"],["L1",5,1,0,4],["DH",4,1,"s"],["BW",[2,1,0],0,256],["L1",6,1,0,4],["DH",5,1,"s"],["L1",7,1,0,4],["BW",[2,1,0],256,256],["DH",6,1,"s"],["L1",8,1,0,4],["DH",7,1,"s"],["L1",9,1,0,4],["DH",8,1,"s"],["QW",[2,1,0],0,512],["L1",10,1,0,4],["DH",9,1,"s"],["QH",0,0],["L1",11,1,0,4],["DH",10,1,"s"],["QH",1,0],["DH",11,1,"s"],["QH",0,1],["C",0,0],["QH",1,1],["C",1,0],["DC",0,0,"s"],["QH",0,2],["C",2,0],["DC",1,0,"s"],["QH",1,2],["C",3,0],["DC",2,0,"s"],["QH",0,3],["C",4,0],["DC",3,0,"s"],["BW",[2,0,1],0,256],["C",5,0],["DC",4,0,"s"],["C",6,0],["DC",5,0,"s"],["BW",[2,0,1],256,256],["C",7,0],["DC",6,0,"s"],["L1",12,1,0,4],["DC",7,0,"s"],["L1",13,1,0,4],["QW",[2,0,1],0,512],["DH",12,1,"s"],["L1",14,1,0,4],["BW",[2,1,1],0,256],["DH",13,1,"s"],["L1",15,1,0,4],["DH",14,1,"s"],["BW",[2,1,1],256,256],["C",8,0],["DH",15,1,"s"],["C",9,0],["DC",8,0,"s"],["C",10,0],["QH",1,3],["DC",9,0,"s"],["C",11,0],["QW",[2,1,1],0,512],["DC",10,0,"s"],["C",12,0],["DC",11,0,"s"],["C",13,0],["DC",12,0,"s"],["C",14,0],["DC",13,0,"s"],["C",15,0],["DC",14,0,"s"],["C",0,1],["DC",15,0,"s"],["C",1,1],["DC",0,1,"s"],["C",2,1],["DC",1,1,"v"],["C",3,1],["DC",2,1,"s"],["C",4,1],["DC",3,1,"v"],["C",5,1],["DC",4,1,"s"],["C",6,1],["DC",5,1,"v"],["C",7,1],["DC",6,1,"s"],["C",8,1],["DC",7,1,"v"],["C",9,1],["DC",8,1,"s"],["C",10,1],["DC",9,1,"v"],["C",11,1],["DC",10,1,"s"],["C",12,1],["DC",11,1,"v"],["C",13,1],["DC",12,1,"s"],["C",14,1],["DC",13,1,"v"],["C",15,1],["DC",14,1,"s"],["DC",15,1,"v"]],"loads":[["x",0,0,2],["w1",0,0],["w1",1,0],["x",0,2,2],["x",1,0,4],["x",2,0,4],["w1",0,1],["x",3,0,4],["w1",1,1],["w2",0,0],["w2",1,0],["w2",0,1],["w2",1,1]],"hgbufs":7,"xgbufs":3}
-
-
-def make_program():
-    return [tuple(tuple(a) if isinstance(a, list) else a for a in t) for t in PJ["prog"]]
+SCALAR, VECTOR = "scalar", "vector"
+X_COPIES_ON_VECTOR = (5, 7, 10)
+TILES_BEFORE_LAYER2 = 12
 
 
 def tile_sparse_connect_kernel(tc, x, th1, sign1, th2, sign2, relu, out):
+    assert relu == 1, "both relus are always applied"
     nc = tc.nc
-    xv = x.flatten_outer_dims().rearrange("(b p j) d -> b p j d", p=P, j=4)
-    ov = out.flatten_outer_dims().rearrange("(b p j) n -> b p j n", p=P, j=4)
-    w1v = {"t": th1.rearrange("(w q e) f -> w q e f", w=4, e=2), "s": sign1.rearrange("(w q e) f -> w q e f", w=4, e=2)}
-    w2v = {"t": th2.rearrange("(a p) n -> p a n", p=P), "s": sign2.rearrange("(a p) n -> p a n", p=P)}
+    x_blocks = x.flatten_outer_dims().rearrange("(b p j) d -> b p j d", p=P, j=4)
+    out_blocks = out.flatten_outer_dims().rearrange("(b p j) n -> b p j n", p=P, j=4)
+    w1_rows = [t.rearrange("(w q e) f -> w q e f", w=4, e=2) for t in (th1, sign1)]
+    w2_rows = [t.rearrange("(a p) n -> p a n", p=P) for t in (th2, sign2)]
+
     with ExitStack() as ctx:
         raw = ctx.enter_context(tc.tile_pool(name="raw", bufs=1))
         keep = ctx.enter_context(tc.tile_pool(name="keep", bufs=1))
         stage = ctx.enter_context(tc.tile_pool(name="stage", bufs=3))
-        outp = ctx.enter_context(tc.tile_pool(name="outp", bufs=8))
+        store = ctx.enter_context(tc.tile_pool(name="store", bufs=8))
         psum = ctx.enter_context(tc.psum_pool(name="psum", bufs=8))
-        if MANUAL:
-            ctx.enter_context(tc.manual_schedule())
+        ctx.enter_context(tc.manual_schedule())
 
-        ident = raw.tile([P, P], F32, name="ident")
-        make_identity(nc, ident[:])
+        identity = raw.tile([P, P], F32, name="identity")
+        make_identity(nc, identity[:])
 
-        xr = {}
-        wraw = {}
+        x_raw = {}
+        w_raw = {}
 
-        def load_x(b, j0, nj):
-            t = raw.tile([P, nj, 1024], BF16, name="xr%d_%d" % (b, j0))
-            nc.sync.dma_start(out=t[:], in_=xv[b, :, j0:j0 + nj, :])
-            for j in range(nj):
-                xr[4 * b + j0 + j] = t[:, j, :]
+        def load_x(block, first, count):
+            t = raw.tile([P, count, WIDTH], BF16, name="x%d_%d" % (block, first))
+            nc.sync.dma_start(out=t[:], in_=x_blocks[block, :, first:first + count, :])
+            for j in range(count):
+                x_raw[4 * block + first + j] = t[:, j, :]
 
-        def load_w1(g, G):
-            for kind in ("t", "s"):
-                t = raw.tile([P, 4, 512], BF16, name="w1%s%d%d" % (kind, g, G))
+        def load_w1(dp, fh):
+            pair = []
+            for k, rows in enumerate(w1_rows):
+                t = raw.tile([P, PACK, HALF], BF16, name="w1_%d%d%d" % (k, dp, fh))
                 for u in range(2):
-                    nc.sync.dma_start(out=t[:, 2 * u:2 * u + 2, :], in_=w1v[kind][2 * g + u, :, :, 512 * G:512 * G + 512])
-                wraw[(1, g, G, kind)] = t
+                    nc.sync.dma_start(out=t[:, 2 * u:2 * u + 2, :],
+                                      in_=rows[2 * dp + u, :, :, HALF * fh:HALF * (fh + 1)])
+                pair.append(t)
+            w_raw[(1, dp, fh)] = pair
 
-        def load_w2(G, n):
-            for kind in ("t", "s"):
-                t = raw.tile([P, 4, 512], BF16, name="w2%s%d%d" % (kind, G, n))
-                nc.sync.dma_start(out=t[:], in_=w2v[kind][:, 4 * G:4 * G + 4, 512 * n:512 * n + 512])
-                wraw[(2, G, n, kind)] = t
+        def load_w2(fh, nh):
+            pair = []
+            for k, rows in enumerate(w2_rows):
+                t = raw.tile([P, PACK, HALF], BF16, name="w2_%d%d%d" % (k, fh, nh))
+                nc.sync.dma_start(out=t[:], in_=rows[:, PACK * fh:PACK * (fh + 1), HALF * nh:HALF * (nh + 1)])
+                pair.append(t)
+            w_raw[(2, fh, nh)] = pair
 
-        for ld in PJ["loads"]:
-            if ld[0] == "x":
-                load_x(ld[1], ld[2], ld[3])
-            elif ld[0] == "w1":
-                load_w1(ld[1], ld[2])
-            else:
-                load_w2(ld[1], ld[2])
+        load_x(0, 0, 2)
+        load_w1(0, 0)
+        load_w1(1, 0)
+        load_x(0, 2, 2)
+        load_x(1, 0, 4)
+        load_x(2, 0, 4)
+        load_w1(0, 1)
+        load_x(3, 0, 4)
+        load_w1(1, 1)
+        for nh in range(2):
+            for fh in range(2):
+                load_w2(fh, nh)
 
-        wc = {}
-        ws = {}
-        for key in [(1, g, G) for g in range(2) for G in range(2)] + [(2, G, n) for G in range(2) for n in range(2)]:
-            wc[key] = keep.tile([P, 512], U32, name="wc%d%d%d" % key, align_bytes=64)
-            ws[key] = keep.tile([P, 512], U8, name="ws%d%d%d" % key, align_bytes=64)
-        xc = [keep.tile([P, 512], U32, name="xc%d" % k, align_bytes=64) for k in range(8)]
-        xs = [keep.tile([P, 512], U8, name="xs%d" % k, align_bytes=64) for k in range(8)]
-        hc = [[keep.tile([P, 512], U32, name="hc%d%d" % (G, b), align_bytes=64) for b in range(4)] for G in range(2)]
-        hs = [[keep.tile([P, 512], U8, name="hs%d%d" % (G, b), align_bytes=64) for b in range(4)] for G in range(2)]
-        xg = {}
-        hg = {}
-        wg = {}
+        def packed(name):
+            return (keep.tile([P, HALF], U32, name=name + "_words", align_bytes=64),
+                    keep.tile([P, HALF], U8, name=name + "_scales", align_bytes=64))
 
-        def drain_relu(eng, dst, src):
-            if eng == "s":
+        w_mx = {key: packed("w%d%d%d" % key) for key in sorted(w_raw)}
+        x_mx = [packed("x%d" % pair) for pair in range(TILES // 2)]
+        h_mx = {(fh, block): packed("h%d%d" % (fh, block)) for fh in range(2) for block in range(4)}
+        x_bf = {}
+        h_bf = {}
+        w_bf = {}
+        banks = {}
+
+        def new_bank(key):
+            banks[key] = psum.tile([P, HALF], F32, tag="bank", name="bank")
+            return banks[key]
+
+        def quantise(mx, first, count, values):
+            words, scales = mx
+            nc.vector.quantize_mx(out=words[:, first:first + count].bitcast(FP8X4),
+                                  scales=scales[:, first:first + count], in_=values)
+
+        def mx_pass(acc, lhs, lhs_first, rhs, rhs_first, rhs_count, start, stop):
+            nc.tensor.matmul_mx(out=acc,
+                                lhsT=lhs[0][:, lhs_first:lhs_first + P].bitcast(FP8X4),
+                                lhsT_scale=lhs[1][:, lhs_first:lhs_first + P],
+                                rhs=rhs[0][:, rhs_first:rhs_first + rhs_count].bitcast(FP8X4),
+                                rhs_scale=rhs[1][:, rhs_first:rhs_first + rhs_count],
+                                start=start, stop=stop)
+
+        def relu_out_of_psum(engine, dst, src):
+            if engine == SCALAR:
                 nc.scalar.activation(out=dst, in_=src, func=RELU)
             else:
                 nc.vector.tensor_scalar_max(out=dst, in0=src, scalar1=0.0)
 
-        tb = {}
+        def transpose_x(first, count):
+            for i in range(first, first + count):
+                bank = new_bank(("x", i))
+                words = x_raw[i].bitcast(F32)
+                for w in range(4):
+                    nc.tensor.transpose(bank[:, P * w:P * (w + 1)], words[:, P * w:P * (w + 1)], identity[:])
+            for i in range(first, first + count):
+                if i % 2 == 0:
+                    x_bf[i // 2] = stage.tile([P, 2 * 2 * P * PACK], BF16, tag="x_bf", name="x_bf", align_bytes=64)
+                dst = x_bf[i // 2][:].bitcast(F32).rearrange("q (j g r u) -> q j g r u", j=2, g=2, u=2)[:, i % 2]
+                src = banks[("x", i)][:].rearrange("q (g u r) -> q g r u", g=2, u=2)
+                if i in X_COPIES_ON_VECTOR:
+                    nc.vector.tensor_copy(out=dst, in_=src)
+                else:
+                    nc.scalar.copy(out=dst, in_=src)
 
-        def op_T(i):
-            bank = psum.tile([P, 512], F32, tag="bank", name="bank")
-            tb[i] = bank
-            src = xr[i].bitcast(F32)
-            for w in range(4):
-                nc.tensor.transpose(bank[:, 128 * w:128 * w + 128], src[:, 128 * w:128 * w + 128], ident[:])
+        def quantise_x(pair):
+            quantise(x_mx[pair], 0, HALF, x_bf[pair][:])
 
-        def op_warm(key, count):
-            src = wraw[key + ("t",)]
-            bank = psum.tile([P, 512], F32, tag="bank", name="bank")
-            for r in range(count):
-                nc.tensor.matmul(out=bank[:], lhsT=src[:, r % 4, 0:128], rhs=src[:, r % 4, :], start=True, stop=True)
-
-        def op_DT(i, eng):
-            if (i // 2) not in xg:
-                xg[i // 2] = stage.tile([P, 2048], BF16, tag="xg", name="xg", align_bytes=64, bufs=PJ.get("xgbufs", 3))
-            dst = xg[i // 2][:].bitcast(F32).rearrange("q (j g r u) -> q j g r u", j=2, g=2, u=2)[:, i % 2]
-            src2 = tb[i][:].rearrange("q (g u r) -> q g r u", g=2, u=2)
-            if eng == "s":
-                nc.scalar.copy(out=dst, in_=src2)
-            else:
-                nc.vector.tensor_copy(out=dst, in_=src2)
-
-        def op_QX(k):
-            nc.vector.quantize_mx(out=xc[k][:].bitcast(FP8X4), scales=xs[k][:], in_=xg[k][:])
-
-        def op_BW(key, c0, ncol):
-            if key not in wg:
-                wg[key] = stage.tile([P, 512, 4], BF16, tag="wg", name="wg", align_bytes=64)
+        def build_w(key, first, count):
+            if key not in w_bf:
+                w_bf[key] = stage.tile([P, HALF, PACK], BF16, tag="w_bf", name="w_bf", align_bytes=64)
+            theta, sign = w_raw[key]
             nc.vector.scalar_tensor_tensor(
-                out=wg[key][:, c0:c0 + ncol, :],
-                in0=wraw[key + ("t",)][:, :, c0:c0 + ncol].rearrange("q t c -> q c t"),
-                scalar=0.0,
-                in1=wraw[key + ("s",)][:, :, c0:c0 + ncol].rearrange("q t c -> q c t"),
-                op0=MAX, op1=MULT)
+                out=w_bf[key][:, first:first + count, :],
+                in0=theta[:, :, first:first + count].rearrange("q t c -> q c t"), scalar=0.0,
+                in1=sign[:, :, first:first + count].rearrange("q t c -> q c t"), op0=MAX, op1=MULT)
 
-        def op_QW(key, c0, ncol):
-            nc.vector.quantize_mx(out=wc[key][:, c0:c0 + ncol].bitcast(FP8X4), scales=ws[key][:, c0:c0 + ncol],
-                                  in_=wg[key][:, c0:c0 + ncol, :].rearrange("q c t -> q (c t)"))
+        def quantise_w(key, first=0, count=HALF):
+            quantise(w_mx[key], first, count, w_bf[key][:, first:first + count, :].rearrange("q c t -> q (c t)"))
 
-        banks = {}
+        def build_w_in_halves(key):
+            build_w(key, 0, HALF // 2)
+            build_w(key, HALF // 2, HALF // 2)
 
-        def op_L1(i, G, t0=0, t1=4):
-            if t0 == 0:
-                banks[(i, G)] = psum.tile([P, 512], F32, tag="bank", name="bank")
-            bank = banks[(i, G)]
-            for t in range(t0, t1):
-                for g in range(2):
-                    o = ((i % 2) * 2 + g) * 128
-                    nc.tensor.matmul_mx(out=bank[:, 128 * t:128 * t + 128],
-                                        lhsT=wc[(1, g, G)][:, 128 * t:128 * t + 128].bitcast(FP8X4),
-                                        lhsT_scale=ws[(1, g, G)][:, 128 * t:128 * t + 128],
-                                        rhs=xc[i // 2][:, o:o + 128].bitcast(FP8X4),
-                                        rhs_scale=xs[i // 2][:, o:o + 128],
-                                        start=(g == 0), stop=(g == 1))
+        def layer1(i, fh):
+            bank = new_bank(("h", i, fh))
+            for t in range(PACK):
+                for dp in range(2):
+                    mx_pass(bank[:, P * t:P * (t + 1)], w_mx[(1, dp, fh)], P * t,
+                            x_mx[i // 2], P * (2 * (i % 2) + dp), P, dp == 0, dp == 1)
+            if i % 4 == 0:
+                h_bf[(fh, i // 4)] = stage.tile([P, 4, P, PACK], BF16, tag="h_bf", name="h_bf", align_bytes=64, bufs=7)
+            relu_out_of_psum(SCALAR, h_bf[(fh, i // 4)][:, i % 4], bank[:].rearrange("p (t r) -> p r t", t=PACK))
 
-        def op_DH(i, G, eng):
-            if (G, i // 4) not in hg:
-                hg[(G, i // 4)] = stage.tile([P, 4, 128, 4], BF16, tag="hg", name="hg", align_bytes=64, bufs=PJ.get("hgbufs", 5))
-            drain_relu(eng, hg[(G, i // 4)][:, i % 4], banks[(i, G)][:].rearrange("p (t r) -> p r t", t=4))
+        def quantise_h(fh, block):
+            quantise(h_mx[(fh, block)], 0, HALF, h_bf[(fh, block)][:].rearrange("p j r t -> p (j r t)"))
 
-        def op_QH(G, b):
-            nc.vector.quantize_mx(out=hc[G][b][:].bitcast(FP8X4), scales=hs[G][b][:],
-                                  in_=hg[(G, b)][:].rearrange("p j r t -> p (j r t)"))
+        def layer2(i, nh, engine):
+            bank = new_bank(("out", i, nh))
+            for fh in range(2):
+                mx_pass(bank[:], h_mx[(fh, i // 4)], P * (i % 4), w_mx[(2, fh, nh)], 0, HALF, fh == 0, fh == 1)
+            result = store.tile([P, HALF], F32, tag="result", name="result")
+            relu_out_of_psum(engine, result[:], bank[:])
+            nc.sync.dma_start(out=out_blocks[i // 4, :, i % 4, HALF * nh:HALF * (nh + 1)], in_=result[:])
 
-        ob = {}
+        def keep_tensor_engine_busy(key, count):
+            theta = w_raw[key][0]
+            bank = new_bank(("unused", key))
+            for r in range(count):
+                nc.tensor.matmul(out=bank[:], lhsT=theta[:, r % PACK, 0:P], rhs=theta[:, r % PACK, :], start=True, stop=True)
 
-        def op_L2(i, n):
-            bank = psum.tile([P, 512], F32, tag="bank", name="bank")
-            ob[(i, n)] = bank
-            o = (i % 4) * 128
-            for G in range(2):
-                nc.tensor.matmul_mx(out=bank[:], lhsT=hc[G][i // 4][:, o:o + 128].bitcast(FP8X4),
-                                    lhsT_scale=hs[G][i // 4][:, o:o + 128],
-                                    rhs=wc[(2, G, n)][:].bitcast(FP8X4), rhs_scale=ws[(2, G, n)][:],
-                                    start=(G == 0), stop=(G == 1))
+        transpose_x(0, 2)
+        keep_tensor_engine_busy((1, 0, 0), 8)
+        quantise_x(0)
+        build_w((1, 0, 0), 0, HALF)
+        keep_tensor_engine_busy((1, 1, 0), 4)
+        quantise_w((1, 0, 0))
+        build_w_in_halves((1, 1, 0))
+        transpose_x(2, 2)
+        quantise_w((1, 1, 0), 0, HALF // 2)
+        quantise_w((1, 1, 0), HALF // 2, HALF // 2)
+        quantise_x(1)
 
-        def op_DC(i, n, eng):
-            ot = outp.tile([P, 512], F32, tag="ot", name="ot")
-            drain_relu(eng, ot[:], ob[(i, n)][:])
-            nc.sync.dma_start(out=ov[i // 4, :, i % 4, 512 * n:512 * n + 512], in_=ot[:])
+        layer1(0, 0)
+        layer1(1, 0)
+        transpose_x(4, 4)
+        quantise_x(2)
+        quantise_x(3)
+        build_w((1, 0, 1), 0, HALF // 2)
+        layer1(2, 0)
+        layer1(3, 0)
+        transpose_x(8, 4)
+        quantise_x(4)
+        quantise_x(5)
+        build_w((1, 0, 1), HALF // 2, HALF // 2)
+        quantise_w((1, 0, 1))
+        build_w((1, 1, 1), 0, HALF // 2)
+        for i in range(4, 8):
+            layer1(i, 0)
+        transpose_x(12, 4)
+        quantise_x(6)
+        quantise_x(7)
+        build_w((1, 1, 1), HALF // 2, HALF // 2)
+        quantise_w((1, 1, 1))
+        for i in range(8, TILES):
+            layer1(i, 0)
 
-        for ti, tok in enumerate(make_program()):
-            k = tok[0]
-            if k == "T":
-                op_T(tok[1])
-            elif k == "TB":
-                for i in range(tok[1], tok[1] + tok[2]):
-                    op_T(i)
-            elif k == "W":
-                op_warm(tok[1], tok[2])
-            elif k == "DT":
-                op_DT(tok[1], tok[2])
-            elif k == "QX":
-                op_QX(tok[1])
-            elif k == "BW":
-                op_BW(tok[1], tok[2], tok[3])
-            elif k == "QW":
-                op_QW(tok[1], tok[2], tok[3])
-            elif k == "L1":
-                op_L1(tok[1], tok[2], tok[3], tok[4])
-            elif k == "DH":
-                op_DH(tok[1], tok[2], tok[3])
-            elif k == "QH":
-                op_QH(tok[1], tok[2])
-            elif k == "C":
-                op_L2(tok[1], tok[2])
-            else:
-                op_DC(tok[1], tok[2], tok[3])
+        build_w_in_halves((2, 0, 0))
+        quantise_w((2, 0, 0))
+        for i in range(4):
+            layer1(i, 1)
+        build_w_in_halves((2, 1, 0))
+        quantise_w((2, 1, 0))
+        quantise_h(0, 0)
+        quantise_h(1, 0)
+        quantise_h(0, 1)
+        for i in range(4, TILES_BEFORE_LAYER2):
+            layer1(i, 1)
+        quantise_h(1, 1)
+        quantise_h(0, 2)
+        quantise_h(1, 2)
+        quantise_h(0, 3)
+
+        for i in range(8):
+            layer2(i, 0, SCALAR)
+        build_w_in_halves((2, 0, 1))
+        quantise_w((2, 0, 1))
+        build_w_in_halves((2, 1, 1))
+        for i in range(TILES_BEFORE_LAYER2, TILES):
+            layer1(i, 1)
+        quantise_h(1, 3)
+        quantise_w((2, 1, 1))
+        for i in range(8, TILES):
+            layer2(i, 0, SCALAR)
+        for i in range(TILES):
+            layer2(i, 1, VECTOR if i % 2 else SCALAR)

from contextlib import ExitStack

import concourse.mybir as mybir
from concourse.masks import make_identity

F32 = mybir.dt.float32
BF16 = mybir.dt.bfloat16
U32 = mybir.dt.uint32
U8 = mybir.dt.uint8
FP8X4 = mybir.dt.float8_e4m3fn_x4
RELU = mybir.ActivationFunctionType.Relu
MAX = mybir.AluOpType.max
MULT = mybir.AluOpType.mult

P = 128
PACK = 4
HALF = 512
WIDTH = 1024
TILES = 16
FLOPS = 2 * 2 * TILES * P * WIDTH * WIDTH

SCALAR, VECTOR = "scalar", "vector"
X_COPIES_ON_VECTOR = (5, 7, 10)
TILES_BEFORE_LAYER2 = 12


def tile_sparse_connect_kernel(tc, x, th1, sign1, th2, sign2, relu, out):
    assert relu == 1, "both relus are always applied"
    nc = tc.nc
    x_blocks = x.flatten_outer_dims().rearrange("(b p j) d -> b p j d", p=P, j=4)
    out_blocks = out.flatten_outer_dims().rearrange("(b p j) n -> b p j n", p=P, j=4)
    w1_rows = [t.rearrange("(w q e) f -> w q e f", w=4, e=2) for t in (th1, sign1)]
    w2_rows = [t.rearrange("(a p) n -> p a n", p=P) for t in (th2, sign2)]

    with ExitStack() as ctx:
        raw = ctx.enter_context(tc.tile_pool(name="raw", bufs=1))
        keep = ctx.enter_context(tc.tile_pool(name="keep", bufs=1))
        stage = ctx.enter_context(tc.tile_pool(name="stage", bufs=3))
        store = ctx.enter_context(tc.tile_pool(name="store", bufs=8))
        psum = ctx.enter_context(tc.psum_pool(name="psum", bufs=8))
        ctx.enter_context(tc.manual_schedule())

        identity = raw.tile([P, P], F32, name="identity")
        make_identity(nc, identity[:])

        x_raw = {}
        w_raw = {}

        def load_x(block, first, count):
            t = raw.tile([P, count, WIDTH], BF16, name="x%d_%d" % (block, first))
            nc.sync.dma_start(out=t[:], in_=x_blocks[block, :, first:first + count, :])
            for j in range(count):
                x_raw[4 * block + first + j] = t[:, j, :]

        def load_w1(dp, fh):
            pair = []
            for k, rows in enumerate(w1_rows):
                t = raw.tile([P, PACK, HALF], BF16, name="w1_%d%d%d" % (k, dp, fh))
                for u in range(2):
                    nc.sync.dma_start(out=t[:, 2 * u:2 * u + 2, :],
                                      in_=rows[2 * dp + u, :, :, HALF * fh:HALF * (fh + 1)])
                pair.append(t)
            w_raw[(1, dp, fh)] = pair

        def load_w2(fh, nh):
            pair = []
            for k, rows in enumerate(w2_rows):
                t = raw.tile([P, PACK, HALF], BF16, name="w2_%d%d%d" % (k, fh, nh))
                nc.sync.dma_start(out=t[:], in_=rows[:, PACK * fh:PACK * (fh + 1), HALF * nh:HALF * (nh + 1)])
                pair.append(t)
            w_raw[(2, fh, nh)] = pair

        load_x(0, 0, 2)
        load_w1(0, 0)
        load_w1(1, 0)
        load_x(0, 2, 2)
        load_x(1, 0, 4)
        load_x(2, 0, 4)
        load_w1(0, 1)
        load_x(3, 0, 4)
        load_w1(1, 1)
        for nh in range(2):
            for fh in range(2):
                load_w2(fh, nh)

        def packed(name):
            return (keep.tile([P, HALF], U32, name=name + "_words", align_bytes=64),
                    keep.tile([P, HALF], U8, name=name + "_scales", align_bytes=64))

        w_mx = {key: packed("w%d%d%d" % key) for key in sorted(w_raw)}
        x_mx = [packed("x%d" % pair) for pair in range(TILES // 2)]
        h_mx = {(fh, block): packed("h%d%d" % (fh, block)) for fh in range(2) for block in range(4)}
        x_bf = {}
        h_bf = {}
        w_bf = {}
        banks = {}

        def new_bank(key):
            banks[key] = psum.tile([P, HALF], F32, tag="bank", name="bank")
            return banks[key]

        def quantise(mx, first, count, values):
            words, scales = mx
            nc.vector.quantize_mx(out=words[:, first:first + count].bitcast(FP8X4),
                                  scales=scales[:, first:first + count], in_=values)

        def mx_pass(acc, lhs, lhs_first, rhs, rhs_first, rhs_count, start, stop):
            nc.tensor.matmul_mx(out=acc,
                                lhsT=lhs[0][:, lhs_first:lhs_first + P].bitcast(FP8X4),
                                lhsT_scale=lhs[1][:, lhs_first:lhs_first + P],
                                rhs=rhs[0][:, rhs_first:rhs_first + rhs_count].bitcast(FP8X4),
                                rhs_scale=rhs[1][:, rhs_first:rhs_first + rhs_count],
                                start=start, stop=stop)

        def relu_out_of_psum(engine, dst, src):
            if engine == SCALAR:
                nc.scalar.activation(out=dst, in_=src, func=RELU)
            else:
                nc.vector.tensor_scalar_max(out=dst, in0=src, scalar1=0.0)

        def transpose_x(first, count):
            for i in range(first, first + count):
                bank = new_bank(("x", i))
                words = x_raw[i].bitcast(F32)
                for w in range(4):
                    nc.tensor.transpose(bank[:, P * w:P * (w + 1)], words[:, P * w:P * (w + 1)], identity[:])
            for i in range(first, first + count):
                if i % 2 == 0:
                    x_bf[i // 2] = stage.tile([P, 2 * 2 * P * PACK], BF16, tag="x_bf", name="x_bf", align_bytes=64)
                dst = x_bf[i // 2][:].bitcast(F32).rearrange("q (j g r u) -> q j g r u", j=2, g=2, u=2)[:, i % 2]
                src = banks[("x", i)][:].rearrange("q (g u r) -> q g r u", g=2, u=2)
                if i in X_COPIES_ON_VECTOR:
                    nc.vector.tensor_copy(out=dst, in_=src)
                else:
                    nc.scalar.copy(out=dst, in_=src)

        def quantise_x(pair):
            quantise(x_mx[pair], 0, HALF, x_bf[pair][:])

        def build_w(key, first, count):
            if key not in w_bf:
                w_bf[key] = stage.tile([P, HALF, PACK], BF16, tag="w_bf", name="w_bf", align_bytes=64)
            theta, sign = w_raw[key]
            nc.vector.scalar_tensor_tensor(
                out=w_bf[key][:, first:first + count, :],
                in0=theta[:, :, first:first + count].rearrange("q t c -> q c t"), scalar=0.0,
                in1=sign[:, :, first:first + count].rearrange("q t c -> q c t"), op0=MAX, op1=MULT)

        def quantise_w(key, first=0, count=HALF):
            quantise(w_mx[key], first, count, w_bf[key][:, first:first + count, :].rearrange("q c t -> q (c t)"))

        def build_w_in_halves(key):
            build_w(key, 0, HALF // 2)
            build_w(key, HALF // 2, HALF // 2)

        def layer1(i, fh):
            bank = new_bank(("h", i, fh))
            for t in range(PACK):
                for dp in range(2):
                    mx_pass(bank[:, P * t:P * (t + 1)], w_mx[(1, dp, fh)], P * t,
                            x_mx[i // 2], P * (2 * (i % 2) + dp), P, dp == 0, dp == 1)
            if i % 4 == 0:
                h_bf[(fh, i // 4)] = stage.tile([P, 4, P, PACK], BF16, tag="h_bf", name="h_bf", align_bytes=64, bufs=7)
            relu_out_of_psum(SCALAR, h_bf[(fh, i // 4)][:, i % 4], bank[:].rearrange("p (t r) -> p r t", t=PACK))

        def quantise_h(fh, block):
            quantise(h_mx[(fh, block)], 0, HALF, h_bf[(fh, block)][:].rearrange("p j r t -> p (j r t)"))

        def layer2(i, nh, engine):
            bank = new_bank(("out", i, nh))
            for fh in range(2):
                mx_pass(bank[:], h_mx[(fh, i // 4)], P * (i % 4), w_mx[(2, fh, nh)], 0, HALF, fh == 0, fh == 1)
            result = store.tile([P, HALF], F32, tag="result", name="result")
            relu_out_of_psum(engine, result[:], bank[:])
            nc.sync.dma_start(out=out_blocks[i // 4, :, i % 4, HALF * nh:HALF * (nh + 1)], in_=result[:])

        def keep_tensor_engine_busy(key, count):
            theta = w_raw[key][0]
            bank = new_bank(("unused", key))
            for r in range(count):
                nc.tensor.matmul(out=bank[:], lhsT=theta[:, r % PACK, 0:P], rhs=theta[:, r % PACK, :], start=True, stop=True)

        transpose_x(0, 2)
        keep_tensor_engine_busy((1, 0, 0), 8)
        quantise_x(0)
        build_w((1, 0, 0), 0, HALF)
        keep_tensor_engine_busy((1, 1, 0), 4)
        quantise_w((1, 0, 0))
        build_w_in_halves((1, 1, 0))
        transpose_x(2, 2)
        quantise_w((1, 1, 0), 0, HALF // 2)
        quantise_w((1, 1, 0), HALF // 2, HALF // 2)
        quantise_x(1)

        layer1(0, 0)
        layer1(1, 0)
        transpose_x(4, 4)
        quantise_x(2)
        quantise_x(3)
        build_w((1, 0, 1), 0, HALF // 2)
        layer1(2, 0)
        layer1(3, 0)
        transpose_x(8, 4)
        quantise_x(4)
        quantise_x(5)
        build_w((1, 0, 1), HALF // 2, HALF // 2)
        quantise_w((1, 0, 1))
        build_w((1, 1, 1), 0, HALF // 2)
        for i in range(4, 8):
            layer1(i, 0)
        transpose_x(12, 4)
        quantise_x(6)
        quantise_x(7)
        build_w((1, 1, 1), HALF // 2, HALF // 2)
        quantise_w((1, 1, 1))
        for i in range(8, TILES):
            layer1(i, 0)

        build_w_in_halves((2, 0, 0))
        quantise_w((2, 0, 0))
        for i in range(4):
            layer1(i, 1)
        build_w_in_halves((2, 1, 0))
        quantise_w((2, 1, 0))
        quantise_h(0, 0)
        quantise_h(1, 0)
        quantise_h(0, 1)
        for i in range(4, TILES_BEFORE_LAYER2):
            layer1(i, 1)
        quantise_h(1, 1)
        quantise_h(0, 2)
        quantise_h(1, 2)
        quantise_h(0, 3)

        for i in range(8):
            layer2(i, 0, SCALAR)
        build_w_in_halves((2, 0, 1))
        quantise_w((2, 0, 1))
        build_w_in_halves((2, 1, 1))
        for i in range(TILES_BEFORE_LAYER2, TILES):
            layer1(i, 1)
        quantise_h(1, 3)
        quantise_w((2, 1, 1))
        for i in range(8, TILES):
            layer2(i, 0, SCALAR)
        for i in range(TILES):
            layer2(i, 1, VECTOR if i % 2 else SCALAR)
